import numpy as np
import ml_dtypes


def mxq(x, axis, fmt="e4m3"):
    dtype, down = {"e4m3": (ml_dtypes.float8_e4m3fn, 7), "e5m2": (ml_dtypes.float8_e5m2, 14)}[fmt]
    v = np.moveaxis(np.asarray(x, np.float32).astype(ml_dtypes.bfloat16).astype(np.float64), axis, -1)
    blocks = v.reshape(v.shape[:-1] + (-1, 32))
    amax = np.abs(blocks).max(-1, keepdims=True)
    byte = np.maximum(np.where(amax > 0, np.frexp(amax)[1] - 1 + 127, 0) - down, 1)
    scale = np.exp2(byte - 127.0)
    codes = (blocks / scale).astype(np.float32).astype(dtype).astype(np.float64)
    return np.moveaxis((codes * scale).reshape(v.shape), -1, axis)


BF16 = ml_dtypes.bfloat16


def bf(x):
    return np.asarray(x, np.float32).astype(BF16)


def f64(x):
    return np.asarray(x).astype(np.float64)


B, D, N, R = 128, 1024, 1024, 8
EPS = 1e-8


def draw_rows(m, p):
    v = np.random.standard_normal((m, R)) @ p / np.sqrt(R) + 0.5 * np.random.standard_normal((m, D))
    tiny = np.random.random(m) < 0.125
    return v * np.where(tiny, 0.4 * EPS / np.sqrt(D), 1.0)[:, None]


def setup_inputs():
    p = np.random.standard_normal((R, D))
    return {"features": bf(draw_rows(B, p)), "weight": bf(draw_rows(N, p)),
            "threshold": bf(0.5 + 0.1 * np.random.standard_normal(1))}


def reference(features, weight, threshold):
    features, weight = f64(features), f64(weight)
    f_norm = np.sqrt((features ** 2).sum(axis=1, keepdims=True))
    w_norm = np.sqrt((weight ** 2).sum(axis=1, keepdims=True))
    f_hat = features / np.maximum(f_norm, EPS)
    w_hat = weight / np.maximum(w_norm, EPS)
    sim_mt = mxq(f_hat, 1, "e4m3") @ mxq(w_hat, 1, "e4m3").T
    cui_less = np.full((features.shape[0], 1), 1.0) * f64(threshold)
    return np.concatenate([sim_mt, cui_less], axis=1)

@@ -1,0 +1,121 @@
+from contextlib import ExitStack
+
+import concourse.mybir as mybir
+from concourse.masks import make_identity
+
+F32 = mybir.dt.float32
+BF16 = mybir.dt.bfloat16
+U32 = mybir.dt.uint32
+U8 = mybir.dt.uint8
+FP8X4 = mybir.dt.float8_e4m3fn_x4
+ALU = mybir.AluOpType
+ACT = mybir.ActivationFunctionType
+
+P = 128
+K = 1024
+N = 1024
+PACK = 4
+PASSES = K // (P * PACK)
+PAIRS = PACK // 2
+EPS = 1e-8
+STORE_TILES = 2
+AHEAD = 2
+
+FLOPS = 2 * P * N * K
+
+
+def tile_cosinelayer_s_kernel(tc, features, weight, threshold, out):
+    nc = tc.nc
+    weight_tiles = N // P
+    dram_rows = [features] + [weight[j * P : (j + 1) * P, :] for j in range(weight_tiles)]
+    n_tiles = len(dram_rows)
+
+    with ExitStack() as ctx:
+        consts = ctx.enter_context(tc.tile_pool(name="consts", bufs=1))
+        work = ctx.enter_context(tc.tile_pool(name="work", bufs=n_tiles))
+        turned_banks = ctx.enter_context(tc.psum_pool(name="turned_banks", bufs=4))
+        product_banks = ctx.enter_context(tc.psum_pool(name="product_banks", bufs=3))
+
+        threshold_bf16 = consts.tile([P, 1], BF16)
+        nc.scalar.dma_start(out=threshold_bf16[:], in_=threshold.partition_broadcast(P))
+
+        raw = []
+        for rows in dram_rows:
+            raw_rows = work.tile([P, K], BF16)
+            nc.sync.dma_start(out=raw_rows[:], in_=rows)
+            raw.append(raw_rows)
+
+        identity = consts.tile([P, P], F32)
+        make_identity(nc, identity[:])
+        minus_half = consts.tile([P, 1], F32)
+        nc.gpsimd.memset(minus_half[:], -0.5)
+
+        result = consts.tile([P, N + 1], F32)
+        nc.gpsimd.tensor_copy(out=result[:, N : N + 1], in_=threshold_bf16[:])
+
+        def inverse_norm_of(i):
+            squares = work.tile([P, K], BF16)
+            square_sum = work.tile([P, 1], F32)
+            nc.scalar.activation(out=squares[:], in_=raw[i][:], func=ACT.Square, accum_out=square_sum[:])
+            bounded_sum = work.tile([P, 1], F32)
+            nc.gpsimd.tensor_scalar(
+                out=bounded_sum[:], in0=square_sum[:], scalar1=EPS * EPS, scalar2=None, op0=ALU.max
+            )
+            inverse_norm = work.tile([P, 1], F32)
+            nc.gpsimd.tensor_tensor(out=inverse_norm[:], in0=bounded_sum[:], in1=minus_half[:], op=ALU.pow)
+            return inverse_norm
+
+        def turn(i, inverse_norm):
+            unit_rows = work.tile([P, K], BF16)
+            nc.vector.tensor_scalar(
+                out=unit_rows[:], in0=raw[i][:], scalar1=inverse_norm[:, 0:1], scalar2=None, op0=ALU.mult
+            )
+            unit_words = unit_rows[:].bitcast(F32)
+            turned = turned_banks.tile([P, PASSES * PAIRS, P], F32)
+            for c in range(PASSES * PAIRS):
+                nc.tensor.transpose(turned[:, c, :], unit_words[:, c * P : (c + 1) * P], identity[:])
+            return turned
+
+        def quantise(turned):
+            grouped = work.tile([P, K], BF16, align_bytes=64)
+            nc.vector.tensor_copy(
+                out=grouped[:].bitcast(F32).rearrange("p (g r u) -> p g r u", g=PASSES, u=PAIRS),
+                in_=turned[:].rearrange("p (g u) r -> p g r u", u=PAIRS),
+            )
+            codes = work.tile([P, PASSES * P], U32, align_bytes=64)
+            scales = work.tile([P, PASSES * P], U8, align_bytes=64)
+            nc.vector.quantize_mx(out=codes[:].bitcast(FP8X4), scales=scales[:], in_=grouped[:])
+            return codes, scales
+
+        def multiply(j, feature_operand, weight_operand):
+            feature_codes, feature_scales = feature_operand
+            weight_codes, weight_scales = weight_operand
+            product = product_banks.tile([P, P], F32)
+            for g in range(PASSES):
+                of_pass = slice(g * P, (g + 1) * P)
+                nc.tensor.matmul_mx(
+                    out=product[:],
+                    lhsT=feature_codes[:, of_pass].bitcast(FP8X4),
+                    lhsT_scale=feature_scales[:, of_pass],
+                    rhs=weight_codes[:, of_pass].bitcast(FP8X4),
+                    rhs_scale=weight_scales[:, of_pass],
+                    start=(g == 0),
+                    stop=(g == PASSES - 1),
+                )
+            nc.scalar.copy(out=result[:, j * P : (j + 1) * P], in_=product[:])
+            if (j + 1) % STORE_TILES == 0:
+                first = (j + 1 - STORE_TILES) * P
+                end = N + 1 if j == weight_tiles - 1 else (j + 1) * P
+                nc.sync.dma_start(out=out[:, first:end], in_=result[:, first:end])
+
+        inverse_norms = [inverse_norm_of(i) for i in range(n_tiles)]
+        turned_tiles = []
+        operands = []
+        for step in range(n_tiles + AHEAD):
+            if step < n_tiles:
+                turned_tiles.append(turn(step, inverse_norms[step]))
+            i = step - AHEAD
+            if i >= 0:
+                operands.append(quantise(turned_tiles[i]))
+            if i >= 1:
+                multiply(i - 1, operands[0], operands[i])

@@ -18,8 +18,7 @@ PACK = 4
 PASSES = K // (P * PACK)
 PAIRS = PACK // 2
 EPS = 1e-8
-STORE_TILES = 2
-AHEAD = 2
+CHUNKS = (4, 3, 1)
 
 FLOPS = 2 * P * N * K
 
@@ -27,74 +26,106 @@ FLOPS = 2 * P * N * K
 def tile_cosinelayer_s_kernel(tc, features, weight, threshold, out):
     nc = tc.nc
     weight_tiles = N // P
-    dram_rows = [features] + [weight[j * P : (j + 1) * P, :] for j in range(weight_tiles)]
+    dram_rows = [features] + [weight[j * P : (j + 1) * P, :] for j in reversed(range(weight_tiles))]
     n_tiles = len(dram_rows)
 
     with ExitStack() as ctx:
         consts = ctx.enter_context(tc.tile_pool(name="consts", bufs=1))
         work = ctx.enter_context(tc.tile_pool(name="work", bufs=n_tiles))
-        turned_banks = ctx.enter_context(tc.psum_pool(name="turned_banks", bufs=4))
+        turned_banks = ctx.enter_context(tc.psum_pool(name="turned_banks", bufs=5))
         product_banks = ctx.enter_context(tc.psum_pool(name="product_banks", bufs=3))
-
-        threshold_bf16 = consts.tile([P, 1], BF16)
-        nc.scalar.dma_start(out=threshold_bf16[:], in_=threshold.partition_broadcast(P))
+        ctx.enter_context(tc.manual_schedule())
 
         raw = []
         for rows in dram_rows:
             raw_rows = work.tile([P, K], BF16)
             nc.sync.dma_start(out=raw_rows[:], in_=rows)
             raw.append(raw_rows)
+        threshold_bf16 = consts.tile([P, 1], BF16)
+        nc.sync.dma_start(out=threshold_bf16[:], in_=threshold.partition_broadcast(P))
 
+        one = consts.tile([P, 1], F32)
+        nc.gpsimd.memset(one[:], 1.0)
         identity = consts.tile([P, P], F32)
         make_identity(nc, identity[:])
-        minus_half = consts.tile([P, 1], F32)
-        nc.gpsimd.memset(minus_half[:], -0.5)
+        warm = consts.tile([P, 1], F32)
+        nc.scalar.activation(out=warm[:], in_=one[:], func=ACT.Sqrt)
 
         result = consts.tile([P, N + 1], F32)
-        nc.gpsimd.tensor_copy(out=result[:, N : N + 1], in_=threshold_bf16[:])
+        square_sums = [work.tile([P, 2], F32, name="square_sums") for g in range((n_tiles + 1) // 2)]
+        norms = {}
+        bounded_norms = {}
+        inverse_norms = {}
+        turned_tiles = {}
+        grouped_tiles = {}
+        operands = {}
 
-        def inverse_norm_of(i):
+        def square(i):
             squares = work.tile([P, K], BF16)
-            square_sum = work.tile([P, 1], F32)
-            nc.scalar.activation(out=squares[:], in_=raw[i][:], func=ACT.Square, accum_out=square_sum[:])
-            bounded_sum = work.tile([P, 1], F32)
-            nc.gpsimd.tensor_scalar(
-                out=bounded_sum[:], in0=square_sum[:], scalar1=EPS * EPS, scalar2=None, op0=ALU.max
-            )
-            inverse_norm = work.tile([P, 1], F32)
-            nc.gpsimd.tensor_tensor(out=inverse_norm[:], in0=bounded_sum[:], in1=minus_half[:], op=ALU.pow)
-            return inverse_norm
+            total = square_sums[i // 2][:, i % 2 : i % 2 + 1]
+            if i % 2 == 0:
+                nc.scalar.activation(out=squares[:], in_=raw[i][:], func=ACT.Square, accum_out=total)
+            else:
+                nc.vector.scalar_tensor_tensor(
+                    out=squares[:], in0=raw[i][:], scalar=1.0, in1=raw[i][:], op0=ALU.mult, op1=ALU.mult, accum_out=total
+                )
 
-        def turn(i, inverse_norm):
+        def width(g):
+            return min(2, n_tiles - 2 * g)
+
+        def root(g):
+            norm = work.tile([P, 2], F32)
+            nc.scalar.activation(out=norm[:, : width(g)], in_=square_sums[g][:, : width(g)], func=ACT.Sqrt)
+            norms[g] = norm
+
+        def bound(g):
+            bounded = work.tile([P, 2], F32)
+            nc.vector.tensor_scalar(
+                out=bounded[:, : width(g)], in0=norms[g][:, : width(g)], scalar1=EPS, scalar2=None, op0=ALU.max
+            )
+            bounded_norms[g] = bounded
+
+        def invert(g):
+            inverse = work.tile([P, 2], F32)
+            nc.vector.reciprocal(out=inverse[:, : width(g)], in_=bounded_norms[g][:, : width(g)])
+            inverse_norms[g] = inverse
+
+        def turn(i):
             unit_rows = work.tile([P, K], BF16)
             nc.vector.tensor_scalar(
-                out=unit_rows[:], in0=raw[i][:], scalar1=inverse_norm[:, 0:1], scalar2=None, op0=ALU.mult
+                out=unit_rows[:],
+                in0=raw[i][:],
+                scalar1=inverse_norms[i // 2][:, i % 2 : i % 2 + 1],
+                scalar2=None,
+                op0=ALU.mult,
             )
             unit_words = unit_rows[:].bitcast(F32)
             turned = turned_banks.tile([P, PASSES * PAIRS, P], F32)
             for c in range(PASSES * PAIRS):
                 nc.tensor.transpose(turned[:, c, :], unit_words[:, c * P : (c + 1) * P], identity[:])
-            return turned
+            turned_tiles[i] = turned
 
-        def quantise(turned):
+        def group(i):
             grouped = work.tile([P, K], BF16, align_bytes=64)
-            nc.vector.tensor_copy(
+            nc.scalar.copy(
                 out=grouped[:].bitcast(F32).rearrange("p (g r u) -> p g r u", g=PASSES, u=PAIRS),
-                in_=turned[:].rearrange("p (g u) r -> p g r u", u=PAIRS),
+                in_=turned_tiles[i][:].rearrange("p (g u) r -> p g r u", u=PAIRS),
             )
+            grouped_tiles[i] = grouped
+
+        def quantise(i):
             codes = work.tile([P, PASSES * P], U32, align_bytes=64)
             scales = work.tile([P, PASSES * P], U8, align_bytes=64)
-            nc.vector.quantize_mx(out=codes[:].bitcast(FP8X4), scales=scales[:], in_=grouped[:])
-            return codes, scales
+            nc.vector.quantize_mx(out=codes[:].bitcast(FP8X4), scales=scales[:], in_=grouped_tiles[i][:])
+            operands[i] = (codes, scales)
 
-        def multiply(j, feature_operand, weight_operand):
-            feature_codes, feature_scales = feature_operand
-            weight_codes, weight_scales = weight_operand
-            product = product_banks.tile([P, P], F32)
+        def multiply(i, product, column):
+            feature_codes, feature_scales = operands[0]
+            weight_codes, weight_scales = operands[i]
             for g in range(PASSES):
                 of_pass = slice(g * P, (g + 1) * P)
                 nc.tensor.matmul_mx(
-                    out=product[:],
+                    out=product[:, column : column + P],
                     lhsT=feature_codes[:, of_pass].bitcast(FP8X4),
                     lhsT_scale=feature_scales[:, of_pass],
                     rhs=weight_codes[:, of_pass].bitcast(FP8X4),
@@ -102,20 +133,57 @@ def tile_cosinelayer_s_kernel(tc, features, weight, threshold, out):
                     start=(g == 0),
                     stop=(g == PASSES - 1),
                 )
-            nc.scalar.copy(out=result[:, j * P : (j + 1) * P], in_=product[:])
-            if (j + 1) % STORE_TILES == 0:
-                first = (j + 1 - STORE_TILES) * P
-                end = N + 1 if j == weight_tiles - 1 else (j + 1) * P
-                nc.sync.dma_start(out=out[:, first:end], in_=result[:, first:end])
 
-        inverse_norms = [inverse_norm_of(i) for i in range(n_tiles)]
-        turned_tiles = []
-        operands = []
-        for step in range(n_tiles + AHEAD):
-            if step < n_tiles:
-                turned_tiles.append(turn(step, inverse_norms[step]))
-            i = step - AHEAD
-            if i >= 0:
-                operands.append(quantise(turned_tiles[i]))
-            if i >= 1:
-                multiply(i - 1, operands[0], operands[i])
+        n_groups = len(square_sums)
+        grouped_next = 0
+        for g in range(n_groups + 2):
+            for i in (2 * g, 2 * g + 1):
+                if i < n_tiles:
+                    square(i)
+            if 1 <= g <= n_groups:
+                root(g - 1)
+                bound(g - 1)
+            if g >= 2 and 2 * (g - 2) < n_tiles:
+                turn(2 * (g - 2))
+            if 1 <= g <= n_groups:
+                invert(g - 1)
+            if g >= 2 and 2 * (g - 2) + 1 < n_tiles:
+                turn(2 * (g - 2) + 1)
+            if g >= n_groups - 1:
+                for i in range(2):
+                    group(grouped_next)
+                    grouped_next += 1
+                if g >= n_groups:
+                    quantise(2 * (g - n_groups))
+                    quantise(2 * (g - n_groups) + 1)
+        nc.scalar.copy(out=result[:, N : N + 1], in_=threshold_bf16[:])
+
+        chunk_of = {}
+        first = 1
+        for size in CHUNKS:
+            for i in range(first, first + size):
+                chunk_of[i] = (first, size)
+            first += size
+        quantised_next = 4
+        products = {}
+        for i in range(1, n_tiles):
+            if grouped_next < n_tiles:
+                group(grouped_next)
+                grouped_next += 1
+            if quantised_next < n_tiles:
+                quantise(quantised_next)
+                quantised_next += 1
+            first, size = chunk_of[i]
+            if i == first:
+                product = product_banks.tile([P, size * P], F32)
+                products[first] = product
+            multiply(i, products[first], (first + size - 1 - i) * P)
+            if i == first + size - 1:
+                begin = (weight_tiles - i) * P
+                end = begin + size * P
+                if first == 1:
+                    nc.vector.tensor_copy(out=result[:, begin:end], in_=products[first][:])
+                else:
+                    nc.scalar.copy(out=result[:, begin:end], in_=products[first][:])
+                last = N + 1 if end == N else end
+                nc.sync.dma_start(out=out[:, begin:last], in_=result[:, begin:last])

@@ -49,12 +49,13 @@ def tile_cosinelayer_s_kernel(tc, features, weight, threshold, out):
         identity = consts.tile([P, P], F32)
         make_identity(nc, identity[:])
         warm = consts.tile([P, 1], F32)
-        nc.scalar.activation(out=warm[:], in_=one[:], func=ACT.Sqrt)
+        nc.scalar.activation(out=warm[:], in_=one[:], func=ACT.Abs_reciprocal_sqrt)
 
         result = consts.tile([P, N + 1], F32)
-        square_sums = [work.tile([P, 2], F32, name="square_sums") for g in range((n_tiles + 1) // 2)]
-        norms = {}
-        bounded_norms = {}
+        groups = [(0, 1), (2, 3), (4, 5), (6, 7, 8)]
+        place = {i: (g, c) for g, tiles in enumerate(groups) for c, i in enumerate(tiles)}
+        square_sums = [work.tile([P, len(tiles)], F32, name="square_sums") for tiles in groups]
+        excesses = {}
         inverse_norms = {}
         turned_tiles = {}
         grouped_tiles = {}
@@ -62,7 +63,8 @@ def tile_cosinelayer_s_kernel(tc, features, weight, threshold, out):
 
         def square(i):
             squares = work.tile([P, K], BF16)
-            total = square_sums[i // 2][:, i % 2 : i % 2 + 1]
+            g, c = place[i]
+            total = square_sums[g][:, c : c + 1]
             if i % 2 == 0:
                 nc.scalar.activation(out=squares[:], in_=raw[i][:], func=ACT.Square, accum_out=total)
             else:
@@ -70,24 +72,14 @@ def tile_cosinelayer_s_kernel(tc, features, weight, threshold, out):
                     out=squares[:], in0=raw[i][:], scalar=1.0, in1=raw[i][:], op0=ALU.mult, op1=ALU.mult, accum_out=total
                 )
 
-        def width(g):
-            return min(2, n_tiles - 2 * g)
+        def excess_of(g):
+            excess = work.tile([P, len(groups[g])], F32)
+            nc.scalar.activation(out=excess[:], in_=square_sums[g][:], func=ACT.Relu, bias=-EPS * EPS)
+            excesses[g] = excess
 
         def root(g):
-            norm = work.tile([P, 2], F32)
-            nc.scalar.activation(out=norm[:, : width(g)], in_=square_sums[g][:, : width(g)], func=ACT.Sqrt)
-            norms[g] = norm
-
-        def bound(g):
-            bounded = work.tile([P, 2], F32)
-            nc.vector.tensor_scalar(
-                out=bounded[:, : width(g)], in0=norms[g][:, : width(g)], scalar1=EPS, scalar2=None, op0=ALU.max
-            )
-            bounded_norms[g] = bounded
-
-        def invert(g):
-            inverse = work.tile([P, 2], F32)
-            nc.vector.reciprocal(out=inverse[:, : width(g)], in_=bounded_norms[g][:, : width(g)])
+            inverse = work.tile([P, len(groups[g])], F32)
+            nc.scalar.activation(out=inverse[:], in_=excesses[g][:], func=ACT.Abs_reciprocal_sqrt, bias=EPS * EPS)
             inverse_norms[g] = inverse
 
         def turn(i):
@@ -95,29 +87,46 @@ def tile_cosinelayer_s_kernel(tc, features, weight, threshold, out):
             nc.vector.tensor_scalar(
                 out=unit_rows[:],
                 in0=raw[i][:],
-                scalar1=inverse_norms[i // 2][:, i % 2 : i % 2 + 1],
+                scalar1=inverse_norms[place[i][0]][:, place[i][1] : place[i][1] + 1],
                 scalar2=None,
                 op0=ALU.mult,
             )
             unit_words = unit_rows[:].bitcast(F32)
-            turned = turned_banks.tile([P, PASSES * PAIRS, P], F32)
-            for c in range(PASSES * PAIRS):
-                nc.tensor.transpose(turned[:, c, :], unit_words[:, c * P : (c + 1) * P], identity[:])
-            turned_tiles[i] = turned
+            banks = PASSES if i == n_tiles - 1 else 1
+            blocks = PASSES * PAIRS // banks
+            turned_tiles[i] = []
+            for b in range(banks):
+                turned = turned_banks.tile([P, blocks, P], F32)
+                for c in range(blocks):
+                    w = (b * blocks + c) * P
+                    nc.tensor.transpose(turned[:, c, :], unit_words[:, w : w + P], identity[:])
+                turned_tiles[i].append(turned)
 
-        def group(i):
-            grouped = work.tile([P, K], BF16, align_bytes=64)
-            nc.scalar.copy(
-                out=grouped[:].bitcast(F32).rearrange("p (g r u) -> p g r u", g=PASSES, u=PAIRS),
-                in_=turned_tiles[i][:].rearrange("p (g u) r -> p g r u", u=PAIRS),
+        def group(i, bank=0, copy=nc.scalar.copy):
+            if bank == 0:
+                grouped_tiles[i] = work.tile([P, K], BF16, name="grouped", align_bytes=64)
+            turned = turned_tiles[i][bank]
+            passes = PASSES // len(turned_tiles[i])
+            first_word = bank * passes * PAIRS * P
+            copy(
+                out=grouped_tiles[i][:]
+                .bitcast(F32)[:, first_word : first_word + passes * PAIRS * P]
+                .rearrange("p (g r u) -> p g r u", g=passes, u=PAIRS),
+                in_=turned[:].rearrange("p (g u) r -> p g r u", u=PAIRS),
             )
-            grouped_tiles[i] = grouped
 
-        def quantise(i):
-            codes = work.tile([P, PASSES * P], U32, align_bytes=64)
-            scales = work.tile([P, PASSES * P], U8, align_bytes=64)
-            nc.vector.quantize_mx(out=codes[:].bitcast(FP8X4), scales=scales[:], in_=grouped_tiles[i][:])
-            operands[i] = (codes, scales)
+        def quantise(i, passes=range(PASSES)):
+            if i not in operands:
+                codes = work.tile([P, PASSES * P], U32, align_bytes=64)
+                scales = work.tile([P, PASSES * P], U8, align_bytes=64)
+                operands[i] = (codes, scales)
+            codes, scales = operands[i]
+            a, b = passes[0], passes[-1] + 1
+            nc.vector.quantize_mx(
+                out=codes[:, a * P : b * P].bitcast(FP8X4),
+                scales=scales[:, a * P : b * P],
+                in_=grouped_tiles[i][:, a * P * PACK : b * P * PACK],
+            )
 
         def multiply(i, product, column):
             feature_codes, feature_scales = operands[0]
@@ -134,28 +143,41 @@ def tile_cosinelayer_s_kernel(tc, features, weight, threshold, out):
                     stop=(g == PASSES - 1),
                 )
 
-        n_groups = len(square_sums)
-        grouped_next = 0
-        for g in range(n_groups + 2):
-            for i in (2 * g, 2 * g + 1):
-                if i < n_tiles:
-                    square(i)
-            if 1 <= g <= n_groups:
-                root(g - 1)
-                bound(g - 1)
-            if g >= 2 and 2 * (g - 2) < n_tiles:
-                turn(2 * (g - 2))
-            if 1 <= g <= n_groups:
-                invert(g - 1)
-            if g >= 2 and 2 * (g - 2) + 1 < n_tiles:
-                turn(2 * (g - 2) + 1)
-            if g >= n_groups - 1:
-                for i in range(2):
-                    group(grouped_next)
-                    grouped_next += 1
-                if g >= n_groups:
-                    quantise(2 * (g - n_groups))
-                    quantise(2 * (g - n_groups) + 1)
+        square(0)
+        square(1)
+        square(2)
+        square(3)
+        excess_of(0)
+        square(4)
+        square(5)
+        root(0)
+        excess_of(1)
+        turn(0)
+        turn(1)
+        square(6)
+        root(1)
+        square(7)
+        excess_of(2)
+        square(8)
+        root(2)
+        turn(2)
+        turn(3)
+        group(0)
+        excess_of(3)
+        turn(4)
+        quantise(0)
+        group(1)
+        root(3)
+        turn(5)
+        group(2)
+        quantise(1)
+        turn(6)
+        turn(7)
+        group(3)
+        quantise(2)
+        turn(8)
+        grouped_next = 4
+        quantised_next = 3
         nc.scalar.copy(out=result[:, N : N + 1], in_=threshold_bf16[:])
 
         chunk_of = {}
@@ -164,14 +186,21 @@ def tile_cosinelayer_s_kernel(tc, features, weight, threshold, out):
             for i in range(first, first + size):
                 chunk_of[i] = (first, size)
             first += size
-        quantised_next = 4
+        last = n_tiles - 1
+        while grouped_next < last:
+            group(grouped_next)
+            grouped_next += 1
+        group(last)
         products = {}
         for i in range(1, n_tiles):
-            if grouped_next < n_tiles:
-                group(grouped_next)
-                grouped_next += 1
-            if quantised_next < n_tiles:
+            if quantised_next == last - 1:
+                group(last, bank=1, copy=nc.vector.tensor_copy)
+            if quantised_next < last:
                 quantise(quantised_next)
+                quantised_next += 1
+            elif quantised_next == last:
+                quantise(last, passes=range(1, 2))
+                quantise(last, passes=range(0, 1))
                 quantised_next += 1
             first, size = chunk_of[i]
             if i == first:
@@ -181,9 +210,9 @@ def tile_cosinelayer_s_kernel(tc, features, weight, threshold, out):
             if i == first + size - 1:
                 begin = (weight_tiles - i) * P
                 end = begin + size * P
-                if first == 1:
+                if i == n_tiles - 1:
                     nc.vector.tensor_copy(out=result[:, begin:end], in_=products[first][:])
                 else:
                     nc.scalar.copy(out=result[:, begin:end], in_=products[first][:])
-                last = N + 1 if end == N else end
-                nc.sync.dma_start(out=out[:, begin:last], in_=result[:, begin:last])
+                stored_end = N + 1 if end == N else end
+                nc.sync.dma_start(out=out[:, begin:stored_end], in_=result[:, begin:stored_end])

@@ -19,6 +19,8 @@ PASSES = K // (P * PACK)
 PAIRS = PACK // 2
 EPS = 1e-8
 CHUNKS = (4, 3, 1)
+WARM_TILES = (1, 2, 3)
+WARM_COLUMNS = 256
 
 FLOPS = 2 * P * N * K
 
@@ -143,6 +145,12 @@ def tile_cosinelayer_s_kernel(tc, features, weight, threshold, out):
                     stop=(g == PASSES - 1),
                 )
 
+        for i in WARM_TILES:
+            product = product_banks.tile([P, WARM_COLUMNS], F32)
+            nc.tensor.matmul(
+                out=product[:], lhsT=identity[:], rhs=raw[i][:].bitcast(F32)[:, :WARM_COLUMNS], start=True, stop=True
+            )
+
         square(0)
         square(1)
         square(2)
@@ -178,7 +186,7 @@ def tile_cosinelayer_s_kernel(tc, features, weight, threshold, out):
         turn(8)
         grouped_next = 4
         quantised_next = 3
-        nc.scalar.copy(out=result[:, N : N + 1], in_=threshold_bf16[:])
+        nc.gpsimd.tensor_copy(out=result[:, N : N + 1], in_=threshold_bf16[:])
 
         chunk_of = {}
         first = 1
@@ -210,7 +218,7 @@ def tile_cosinelayer_s_kernel(tc, features, weight, threshold, out):
             if i == first + size - 1:
                 begin = (weight_tiles - i) * P
                 end = begin + size * P
-                if i == n_tiles - 1:
+                if i == n_tiles - 2:
                     nc.vector.tensor_copy(out=result[:, begin:end], in_=products[first][:])
                 else:
                     nc.scalar.copy(out=result[:, begin:end], in_=products[first][:])

@@ -94,41 +94,24 @@ def tile_cosinelayer_s_kernel(tc, features, weight, threshold, out):
                 op0=ALU.mult,
             )
             unit_words = unit_rows[:].bitcast(F32)
-            banks = PASSES if i == n_tiles - 1 else 1
-            blocks = PASSES * PAIRS // banks
-            turned_tiles[i] = []
-            for b in range(banks):
-                turned = turned_banks.tile([P, blocks, P], F32)
-                for c in range(blocks):
-                    w = (b * blocks + c) * P
-                    nc.tensor.transpose(turned[:, c, :], unit_words[:, w : w + P], identity[:])
-                turned_tiles[i].append(turned)
+            turned = turned_banks.tile([P, PASSES * PAIRS, P], F32)
+            for c in range(PASSES * PAIRS):
+                nc.tensor.transpose(turned[:, c, :], unit_words[:, c * P : (c + 1) * P], identity[:])
+            turned_tiles[i] = turned
 
-        def group(i, bank=0, copy=nc.scalar.copy):
-            if bank == 0:
-                grouped_tiles[i] = work.tile([P, K], BF16, name="grouped", align_bytes=64)
-            turned = turned_tiles[i][bank]
-            passes = PASSES // len(turned_tiles[i])
-            first_word = bank * passes * PAIRS * P
+        def group(i, copy=nc.scalar.copy):
+            grouped = work.tile([P, K], BF16, align_bytes=64)
             copy(
-                out=grouped_tiles[i][:]
-                .bitcast(F32)[:, first_word : first_word + passes * PAIRS * P]
-                .rearrange("p (g r u) -> p g r u", g=passes, u=PAIRS),
-                in_=turned[:].rearrange("p (g u) r -> p g r u", u=PAIRS),
+                out=grouped[:].bitcast(F32).rearrange("p (g r u) -> p g r u", g=PASSES, u=PAIRS),
+                in_=turned_tiles[i][:].rearrange("p (g u) r -> p g r u", u=PAIRS),
             )
+            grouped_tiles[i] = grouped
 
-        def quantise(i, passes=range(PASSES)):
-            if i not in operands:
-                codes = work.tile([P, PASSES * P], U32, align_bytes=64)
-                scales = work.tile([P, PASSES * P], U8, align_bytes=64)
-                operands[i] = (codes, scales)
-            codes, scales = operands[i]
-            a, b = passes[0], passes[-1] + 1
-            nc.vector.quantize_mx(
-                out=codes[:, a * P : b * P].bitcast(FP8X4),
-                scales=scales[:, a * P : b * P],
-                in_=grouped_tiles[i][:, a * P * PACK : b * P * PACK],
-            )
+        def quantise(i):
+            codes = work.tile([P, PASSES * P], U32, align_bytes=64)
+            scales = work.tile([P, PASSES * P], U8, align_bytes=64)
+            nc.vector.quantize_mx(out=codes[:].bitcast(FP8X4), scales=scales[:], in_=grouped_tiles[i][:])
+            operands[i] = (codes, scales)
 
         def multiply(i, product, column):
             feature_codes, feature_scales = operands[0]
@@ -194,21 +177,13 @@ def tile_cosinelayer_s_kernel(tc, features, weight, threshold, out):
             for i in range(first, first + size):
                 chunk_of[i] = (first, size)
             first += size
-        last = n_tiles - 1
-        while grouped_next < last:
+        while grouped_next < n_tiles:
             group(grouped_next)
             grouped_next += 1
-        group(last)
         products = {}
         for i in range(1, n_tiles):
-            if quantised_next == last - 1:
-                group(last, bank=1, copy=nc.vector.tensor_copy)
-            if quantised_next < last:
+            if quantised_next < n_tiles:
                 quantise(quantised_next)
-                quantised_next += 1
-            elif quantised_next == last:
-                quantise(last, passes=range(1, 2))
-                quantise(last, passes=range(0, 1))
                 quantised_next += 1
             first, size = chunk_of[i]
             if i == first:
@@ -218,7 +193,7 @@ def tile_cosinelayer_s_kernel(tc, features, weight, threshold, out):
             if i == first + size - 1:
                 begin = (weight_tiles - i) * P
                 end = begin + size * P
-                if i == n_tiles - 2:
+                if i == n_tiles - 1:
                     nc.vector.tensor_copy(out=result[:, begin:end], in_=products[first][:])
                 else:
                     nc.scalar.copy(out=result[:, begin:end], in_=products[first][:])

@@ -18,7 +18,7 @@ PACK = 4
 PASSES = K // (P * PACK)
 PAIRS = PACK // 2
 EPS = 1e-8
-CHUNKS = (4, 3, 1)
+CHUNKS = (4, 2, 2)
 WARM_TILES = (1, 2, 3)
 WARM_COLUMNS = 256
 
@@ -169,7 +169,6 @@ def tile_cosinelayer_s_kernel(tc, features, weight, threshold, out):
         turn(8)
         grouped_next = 4
         quantised_next = 3
-        nc.gpsimd.tensor_copy(out=result[:, N : N + 1], in_=threshold_bf16[:])
 
         chunk_of = {}
         first = 1
@@ -177,11 +176,14 @@ def tile_cosinelayer_s_kernel(tc, features, weight, threshold, out):
             for i in range(first, first + size):
                 chunk_of[i] = (first, size)
             first += size
-        while grouped_next < n_tiles:
+        last = n_tiles - 1
+        while grouped_next < last:
             group(grouped_next)
             grouped_next += 1
         products = {}
         for i in range(1, n_tiles):
+            if quantised_next == last - 2:
+                group(last, copy=nc.vector.tensor_copy)
             if quantised_next < n_tiles:
                 quantise(quantised_next)
                 quantised_next += 1
@@ -193,9 +195,8 @@ def tile_cosinelayer_s_kernel(tc, features, weight, threshold, out):
             if i == first + size - 1:
                 begin = (weight_tiles - i) * P
                 end = begin + size * P
-                if i == n_tiles - 1:
-                    nc.vector.tensor_copy(out=result[:, begin:end], in_=products[first][:])
-                else:
-                    nc.scalar.copy(out=result[:, begin:end], in_=products[first][:])
+                if first == 1:
+                    nc.scalar.copy(out=result[:, N : N + 1], in_=threshold_bf16[:])
+                nc.scalar.copy(out=result[:, begin:end], in_=products[first][:])
                 stored_end = N + 1 if end == N else end
                 nc.sync.dma_start(out=out[:, begin:stored_end], in_=result[:, begin:stored_end])

@@ -19,8 +19,6 @@ PASSES = K // (P * PACK)
 PAIRS = PACK // 2
 EPS = 1e-8
 CHUNKS = (4, 2, 2)
-WARM_TILES = (1, 2, 3)
-WARM_COLUMNS = 256
 
 FLOPS = 2 * P * N * K
 
@@ -127,12 +125,6 @@ def tile_cosinelayer_s_kernel(tc, features, weight, threshold, out):
                     start=(g == 0),
                     stop=(g == PASSES - 1),
                 )
-
-        for i in WARM_TILES:
-            product = product_banks.tile([P, WARM_COLUMNS], F32)
-            nc.tensor.matmul(
-                out=product[:], lhsT=identity[:], rhs=raw[i][:].bitcast(F32)[:, :WARM_COLUMNS], start=True, stop=True
-            )
 
         square(0)
         square(1)

@@ -17,6 +17,7 @@ N = 1024
 PACK = 4
 PASSES = K // (P * PACK)
 PAIRS = PACK // 2
+WARM_COLUMNS = 256
 EPS = 1e-8
 CHUNKS = (4, 2, 2)
 
@@ -126,6 +127,13 @@ def tile_cosinelayer_s_kernel(tc, features, weight, threshold, out):
                     stop=(g == PASSES - 1),
                 )
 
+        idle_bank = product_banks.tile([P, WARM_COLUMNS], F32, name="product")
+
+        def keep_warm(i):
+            nc.tensor.matmul(
+                out=idle_bank[:], lhsT=identity[:], rhs=raw[i][:].bitcast(F32)[:, :WARM_COLUMNS], start=True, stop=True
+            )
+
         square(0)
         square(1)
         square(2)
@@ -137,6 +145,7 @@ def tile_cosinelayer_s_kernel(tc, features, weight, threshold, out):
         excess_of(1)
         turn(0)
         turn(1)
+        keep_warm(1)
         square(6)
         root(1)
         square(7)
@@ -148,6 +157,7 @@ def tile_cosinelayer_s_kernel(tc, features, weight, threshold, out):
         group(0)
         excess_of(3)
         turn(4)
+        keep_warm(2)
         quantise(0)
         group(1)
         root(3)
@@ -155,6 +165,7 @@ def tile_cosinelayer_s_kernel(tc, features, weight, threshold, out):
         group(2)
         quantise(1)
         turn(6)
+        keep_warm(3)
         turn(7)
         group(3)
         quantise(2)
@@ -181,7 +192,7 @@ def tile_cosinelayer_s_kernel(tc, features, weight, threshold, out):
                 quantised_next += 1
             first, size = chunk_of[i]
             if i == first:
-                product = product_banks.tile([P, size * P], F32)
+                product = product_banks.tile([P, size * P], F32, name="product")
                 products[first] = product
             multiply(i, products[first], (first + size - 1 - i) * P)
             if i == first + size - 1:

@@ -143,9 +143,10 @@ def tile_cosinelayer_s_kernel(tc, features, weight, threshold, out):
         square(5)
         root(0)
         excess_of(1)
+        keep_warm(1)
         turn(0)
         turn(1)
-        keep_warm(1)
+        keep_warm(2)
         square(6)
         root(1)
         square(7)
@@ -157,7 +158,7 @@ def tile_cosinelayer_s_kernel(tc, features, weight, threshold, out):
         group(0)
         excess_of(3)
         turn(4)
-        keep_warm(2)
+        keep_warm(3)
         quantise(0)
         group(1)
         root(3)
@@ -165,7 +166,6 @@ def tile_cosinelayer_s_kernel(tc, features, weight, threshold, out):
         group(2)
         quantise(1)
         turn(6)
-        keep_warm(3)
         turn(7)
         group(3)
         quantise(2)

@@ -143,7 +143,7 @@ def tile_cosinelayer_s_kernel(tc, features, weight, threshold, out):
         square(5)
         root(0)
         excess_of(1)
-        keep_warm(1)
+        keep_warm(5)
         turn(0)
         turn(1)
         keep_warm(2)

@@ -19,7 +19,7 @@ PASSES = K // (P * PACK)
 PAIRS = PACK // 2
 WARM_COLUMNS = 256
 EPS = 1e-8
-CHUNKS = (4, 2, 2)
+CHUNKS = (4, 2, 1, 1)
 
 FLOPS = 2 * P * N * K
 
@@ -33,8 +33,8 @@ def tile_cosinelayer_s_kernel(tc, features, weight, threshold, out):
     with ExitStack() as ctx:
         consts = ctx.enter_context(tc.tile_pool(name="consts", bufs=1))
         work = ctx.enter_context(tc.tile_pool(name="work", bufs=n_tiles))
-        turned_banks = ctx.enter_context(tc.psum_pool(name="turned_banks", bufs=5))
-        product_banks = ctx.enter_context(tc.psum_pool(name="product_banks", bufs=3))
+        turned_banks = ctx.enter_context(tc.psum_pool(name="turned_banks", bufs=4))
+        product_banks = ctx.enter_context(tc.psum_pool(name="product_banks", bufs=4))
         ctx.enter_context(tc.manual_schedule())
 
         raw = []
@@ -83,7 +83,9 @@ def tile_cosinelayer_s_kernel(tc, features, weight, threshold, out):
             nc.scalar.activation(out=inverse[:], in_=excesses[g][:], func=ACT.Abs_reciprocal_sqrt, bias=EPS * EPS)
             inverse_norms[g] = inverse
 
-        def turn(i):
+        unit_tiles = {}
+
+        def scale(i):
             unit_rows = work.tile([P, K], BF16)
             nc.vector.tensor_scalar(
                 out=unit_rows[:],
@@ -92,11 +94,18 @@ def tile_cosinelayer_s_kernel(tc, features, weight, threshold, out):
                 scalar2=None,
                 op0=ALU.mult,
             )
-            unit_words = unit_rows[:].bitcast(F32)
+            unit_tiles[i] = unit_rows
+
+        def transpose_units(i):
+            unit_words = unit_tiles[i][:].bitcast(F32)
             turned = turned_banks.tile([P, PASSES * PAIRS, P], F32)
             for c in range(PASSES * PAIRS):
                 nc.tensor.transpose(turned[:, c, :], unit_words[:, c * P : (c + 1) * P], identity[:])
             turned_tiles[i] = turned
+
+        def turn(i):
+            scale(i)
+            transpose_units(i)
 
         def group(i, copy=nc.scalar.copy):
             grouped = work.tile([P, K], BF16, align_bytes=64)
@@ -169,7 +178,7 @@ def tile_cosinelayer_s_kernel(tc, features, weight, threshold, out):
         turn(7)
         group(3)
         quantise(2)
-        turn(8)
+        scale(8)
         grouped_next = 4
         quantised_next = 3
 
@@ -195,11 +204,15 @@ def tile_cosinelayer_s_kernel(tc, features, weight, threshold, out):
                 product = product_banks.tile([P, size * P], F32, name="product")
                 products[first] = product
             multiply(i, products[first], (first + size - 1 - i) * P)
+            if i == 2:
+                transpose_units(last)
             if i == first + size - 1:
                 begin = (weight_tiles - i) * P
                 end = begin + size * P
                 if first == 1:
                     nc.scalar.copy(out=result[:, N : N + 1], in_=threshold_bf16[:])
-                nc.scalar.copy(out=result[:, begin:end], in_=products[first][:])
-                stored_end = N + 1 if end == N else end
-                nc.sync.dma_start(out=out[:, begin:stored_end], in_=result[:, begin:stored_end])
+                copy = nc.vector.tensor_copy if i == last - 1 else nc.scalar.copy
+                copy(out=result[:, begin:end], in_=products[first][:])
+                if i != last - 1:
+                    stored_end = N + 1 if end == N else end if i < last else 2 * P
+                    nc.sync.dma_start(out=out[:, begin:stored_end], in_=result[:, begin:stored_end])

@@ -33,8 +33,8 @@ def tile_cosinelayer_s_kernel(tc, features, weight, threshold, out):
     with ExitStack() as ctx:
         consts = ctx.enter_context(tc.tile_pool(name="consts", bufs=1))
         work = ctx.enter_context(tc.tile_pool(name="work", bufs=n_tiles))
-        turned_banks = ctx.enter_context(tc.psum_pool(name="turned_banks", bufs=4))
-        product_banks = ctx.enter_context(tc.psum_pool(name="product_banks", bufs=4))
+        turned_banks = ctx.enter_context(tc.psum_pool(name="turned_banks", bufs=5))
+        product_banks = ctx.enter_context(tc.psum_pool(name="product_banks", bufs=3))
         ctx.enter_context(tc.manual_schedule())
 
         raw = []
@@ -168,10 +168,10 @@ def tile_cosinelayer_s_kernel(tc, features, weight, threshold, out):
         excess_of(3)
         turn(4)
         keep_warm(3)
+        turn(5)
         quantise(0)
         group(1)
         root(3)
-        turn(5)
         group(2)
         quantise(1)
         turn(6)
@@ -189,13 +189,14 @@ def tile_cosinelayer_s_kernel(tc, features, weight, threshold, out):
                 chunk_of[i] = (first, size)
             first += size
         last = n_tiles - 1
-        while grouped_next < last:
+        while grouped_next < last - 1:
             group(grouped_next)
             grouped_next += 1
         products = {}
         for i in range(1, n_tiles):
             if quantised_next == last - 2:
-                group(last, copy=nc.vector.tensor_copy)
+                group(last - 1, copy=nc.vector.tensor_copy)
+                group(last)
             if quantised_next < n_tiles:
                 quantise(quantised_next)
                 quantised_next += 1

@@ -138,9 +138,13 @@ def tile_cosinelayer_s_kernel(tc, features, weight, threshold, out):
 
         idle_bank = product_banks.tile([P, WARM_COLUMNS], F32, name="product")
 
-        def keep_warm(i):
+        def keep_warm(i, columns=WARM_COLUMNS):
             nc.tensor.matmul(
-                out=idle_bank[:], lhsT=identity[:], rhs=raw[i][:].bitcast(F32)[:, :WARM_COLUMNS], start=True, stop=True
+                out=idle_bank[:, :columns],
+                lhsT=identity[:],
+                rhs=raw[i][:].bitcast(F32)[:, :columns],
+                start=True,
+                stop=True,
             )
 
         square(0)
@@ -152,10 +156,11 @@ def tile_cosinelayer_s_kernel(tc, features, weight, threshold, out):
         square(5)
         root(0)
         excess_of(1)
+        keep_warm(4, columns=128)
         keep_warm(5)
         turn(0)
         turn(1)
-        keep_warm(2)
+        keep_warm(2, columns=176)
         square(6)
         root(1)
         square(7)

@@ -156,11 +156,11 @@ def tile_cosinelayer_s_kernel(tc, features, weight, threshold, out):
         square(5)
         root(0)
         excess_of(1)
-        keep_warm(4, columns=128)
+        keep_warm(4)
         keep_warm(5)
         turn(0)
         turn(1)
-        keep_warm(2, columns=176)
+        keep_warm(2, columns=128)
         square(6)
         root(1)
         square(7)
@@ -172,7 +172,7 @@ def tile_cosinelayer_s_kernel(tc, features, weight, threshold, out):
         group(0)
         excess_of(3)
         turn(4)
-        keep_warm(3)
+        keep_warm(3, columns=176)
         turn(5)
         quantise(0)
         group(1)

@@ -199,7 +199,7 @@ def tile_cosinelayer_s_kernel(tc, features, weight, threshold, out):
             grouped_next += 1
         products = {}
         for i in range(1, n_tiles):
-            if quantised_next == last - 2:
+            if quantised_next == last - 3:
                 group(last - 1, copy=nc.vector.tensor_copy)
                 group(last)
             if quantised_next < n_tiles:
@@ -215,10 +215,10 @@ def tile_cosinelayer_s_kernel(tc, features, weight, threshold, out):
             if i == first + size - 1:
                 begin = (weight_tiles - i) * P
                 end = begin + size * P
-                if first == 1:
-                    nc.scalar.copy(out=result[:, N : N + 1], in_=threshold_bf16[:])
                 copy = nc.vector.tensor_copy if i == last - 1 else nc.scalar.copy
                 copy(out=result[:, begin:end], in_=products[first][:])
+                if first == 1:
+                    nc.scalar.copy(out=result[:, N : N + 1], in_=threshold_bf16[:])
                 if i != last - 1:
                     stored_end = N + 1 if end == N else end if i < last else 2 * P
                     nc.sync.dma_start(out=out[:, begin:stored_end], in_=result[:, begin:stored_end])

from contextlib import ExitStack

import concourse.mybir as mybir
from concourse.masks import make_identity

F32 = mybir.dt.float32
BF16 = mybir.dt.bfloat16
U32 = mybir.dt.uint32
U8 = mybir.dt.uint8
FP8X4 = mybir.dt.float8_e4m3fn_x4
ALU = mybir.AluOpType
ACT = mybir.ActivationFunctionType

P = 128
K = 1024
N = 1024
PACK = 4
PASSES = K // (P * PACK)
PAIRS = PACK // 2
WARM_COLUMNS = 256
EPS = 1e-8
CHUNKS = (4, 2, 1, 1)

FLOPS = 2 * P * N * K


def tile_cosinelayer_s_kernel(tc, features, weight, threshold, out):
    nc = tc.nc
    weight_tiles = N // P
    dram_rows = [features] + [weight[j * P : (j + 1) * P, :] for j in reversed(range(weight_tiles))]
    n_tiles = len(dram_rows)

    with ExitStack() as ctx:
        consts = ctx.enter_context(tc.tile_pool(name="consts", bufs=1))
        work = ctx.enter_context(tc.tile_pool(name="work", bufs=n_tiles))
        turned_banks = ctx.enter_context(tc.psum_pool(name="turned_banks", bufs=5))
        product_banks = ctx.enter_context(tc.psum_pool(name="product_banks", bufs=3))
        ctx.enter_context(tc.manual_schedule())

        raw = []
        for rows in dram_rows:
            raw_rows = work.tile([P, K], BF16)
            nc.sync.dma_start(out=raw_rows[:], in_=rows)
            raw.append(raw_rows)
        threshold_bf16 = consts.tile([P, 1], BF16)
        nc.sync.dma_start(out=threshold_bf16[:], in_=threshold.partition_broadcast(P))

        one = consts.tile([P, 1], F32)
        nc.gpsimd.memset(one[:], 1.0)
        identity = consts.tile([P, P], F32)
        make_identity(nc, identity[:])
        warm = consts.tile([P, 1], F32)
        nc.scalar.activation(out=warm[:], in_=one[:], func=ACT.Abs_reciprocal_sqrt)

        result = consts.tile([P, N + 1], F32)
        groups = [(0, 1), (2, 3), (4, 5), (6, 7, 8)]
        place = {i: (g, c) for g, tiles in enumerate(groups) for c, i in enumerate(tiles)}
        square_sums = [work.tile([P, len(tiles)], F32, name="square_sums") for tiles in groups]
        excesses = {}
        inverse_norms = {}
        turned_tiles = {}
        grouped_tiles = {}
        operands = {}

        def square(i):
            squares = work.tile([P, K], BF16)
            g, c = place[i]
            total = square_sums[g][:, c : c + 1]
            if i % 2 == 0:
                nc.scalar.activation(out=squares[:], in_=raw[i][:], func=ACT.Square, accum_out=total)
            else:
                nc.vector.scalar_tensor_tensor(
                    out=squares[:], in0=raw[i][:], scalar=1.0, in1=raw[i][:], op0=ALU.mult, op1=ALU.mult, accum_out=total
                )

        def excess_of(g):
            excess = work.tile([P, len(groups[g])], F32)
            nc.scalar.activation(out=excess[:], in_=square_sums[g][:], func=ACT.Relu, bias=-EPS * EPS)
            excesses[g] = excess

        def root(g):
            inverse = work.tile([P, len(groups[g])], F32)
            nc.scalar.activation(out=inverse[:], in_=excesses[g][:], func=ACT.Abs_reciprocal_sqrt, bias=EPS * EPS)
            inverse_norms[g] = inverse

        unit_tiles = {}

        def scale(i):
            unit_rows = work.tile([P, K], BF16)
            nc.vector.tensor_scalar(
                out=unit_rows[:],
                in0=raw[i][:],
                scalar1=inverse_norms[place[i][0]][:, place[i][1] : place[i][1] + 1],
                scalar2=None,
                op0=ALU.mult,
            )
            unit_tiles[i] = unit_rows

        def transpose_units(i):
            unit_words = unit_tiles[i][:].bitcast(F32)
            turned = turned_banks.tile([P, PASSES * PAIRS, P], F32)
            for c in range(PASSES * PAIRS):
                nc.tensor.transpose(turned[:, c, :], unit_words[:, c * P : (c + 1) * P], identity[:])
            turned_tiles[i] = turned

        def turn(i):
            scale(i)
            transpose_units(i)

        def group(i, copy=nc.scalar.copy):
            grouped = work.tile([P, K], BF16, align_bytes=64)
            copy(
                out=grouped[:].bitcast(F32).rearrange("p (g r u) -> p g r u", g=PASSES, u=PAIRS),
                in_=turned_tiles[i][:].rearrange("p (g u) r -> p g r u", u=PAIRS),
            )
            grouped_tiles[i] = grouped

        def quantise(i):
            codes = work.tile([P, PASSES * P], U32, align_bytes=64)
            scales = work.tile([P, PASSES * P], U8, align_bytes=64)
            nc.vector.quantize_mx(out=codes[:].bitcast(FP8X4), scales=scales[:], in_=grouped_tiles[i][:])
            operands[i] = (codes, scales)

        def multiply(i, product, column):
            feature_codes, feature_scales = operands[0]
            weight_codes, weight_scales = operands[i]
            for g in range(PASSES):
                of_pass = slice(g * P, (g + 1) * P)
                nc.tensor.matmul_mx(
                    out=product[:, column : column + P],
                    lhsT=feature_codes[:, of_pass].bitcast(FP8X4),
                    lhsT_scale=feature_scales[:, of_pass],
                    rhs=weight_codes[:, of_pass].bitcast(FP8X4),
                    rhs_scale=weight_scales[:, of_pass],
                    start=(g == 0),
                    stop=(g == PASSES - 1),
                )

        idle_bank = product_banks.tile([P, WARM_COLUMNS], F32, name="product")

        def keep_warm(i, columns=WARM_COLUMNS):
            nc.tensor.matmul(
                out=idle_bank[:, :columns],
                lhsT=identity[:],
                rhs=raw[i][:].bitcast(F32)[:, :columns],
                start=True,
                stop=True,
            )

        square(0)
        square(1)
        square(2)
        square(3)
        excess_of(0)
        square(4)
        square(5)
        root(0)
        excess_of(1)
        keep_warm(4)
        keep_warm(5)
        turn(0)
        turn(1)
        keep_warm(2, columns=128)
        square(6)
        root(1)
        square(7)
        excess_of(2)
        square(8)
        root(2)
        turn(2)
        turn(3)
        group(0)
        excess_of(3)
        turn(4)
        keep_warm(3, columns=176)
        turn(5)
        quantise(0)
        group(1)
        root(3)
        group(2)
        quantise(1)
        turn(6)
        turn(7)
        group(3)
        quantise(2)
        scale(8)
        grouped_next = 4
        quantised_next = 3

        chunk_of = {}
        first = 1
        for size in CHUNKS:
            for i in range(first, first + size):
                chunk_of[i] = (first, size)
            first += size
        last = n_tiles - 1
        while grouped_next < last - 1:
            group(grouped_next)
            grouped_next += 1
        products = {}
        for i in range(1, n_tiles):
            if quantised_next == last - 3:
                group(last - 1, copy=nc.vector.tensor_copy)
                group(last)
            if quantised_next < n_tiles:
                quantise(quantised_next)
                quantised_next += 1
            first, size = chunk_of[i]
            if i == first:
                product = product_banks.tile([P, size * P], F32, name="product")
                products[first] = product
            multiply(i, products[first], (first + size - 1 - i) * P)
            if i == 2:
                transpose_units(last)
            if i == first + size - 1:
                begin = (weight_tiles - i) * P
                end = begin + size * P
                copy = nc.vector.tensor_copy if i == last - 1 else nc.scalar.copy
                copy(out=result[:, begin:end], in_=products[first][:])
                if first == 1:
                    nc.scalar.copy(out=result[:, N : N + 1], in_=threshold_bf16[:])
                if i != last - 1:
                    stored_end = N + 1 if end == N else end if i < last else 2 * P
                    nc.sync.dma_start(out=out[:, begin:stored_end], in_=result[:, begin:stored_end])
